import numpy as np
import ml_dtypes


def mxq(x, axis, fmt="e4m3"):
    dtype, down = {"e4m3": (ml_dtypes.float8_e4m3fn, 7), "e5m2": (ml_dtypes.float8_e5m2, 14)}[fmt]
    v = np.moveaxis(np.asarray(x, np.float32).astype(ml_dtypes.bfloat16).astype(np.float64), axis, -1)
    blocks = v.reshape(v.shape[:-1] + (-1, 32))
    amax = np.abs(blocks).max(-1, keepdims=True)
    byte = np.maximum(np.where(amax > 0, np.frexp(amax)[1] - 1 + 127, 0) - down, 1)
    scale = np.exp2(byte - 127.0)
    codes = (blocks / scale).astype(np.float32).astype(dtype).astype(np.float64)
    return np.moveaxis((codes * scale).reshape(v.shape), -1, axis)


WIDE = False


def mx_kscale(k):
    if not WIDE:
        return np.ones(k)
    levels = np.array([10, -10, 5, -5, 0])
    a = np.random.permutation(np.resize(levels, k // 512 * 4)).reshape(k // 512, 4)
    idx = np.arange(k)
    return np.exp2(a[idx // 512, idx % 128 // 32])


BF16 = ml_dtypes.bfloat16


def bf(x):
    return np.asarray(x, np.float32).astype(BF16)


def f64(x):
    return np.asarray(x).astype(np.float64)


E2M1 = np.array([0.0, 0.5, 1.0, 1.5, 2.0, 3.0, 4.0, 6.0, -0.0, -0.5, -1.0, -1.5, -2.0, -3.0, -4.0, -6.0])


def pack_weight(w, fmt):
    k, n = w.shape
    w = f64(bf(w)).reshape(k // 32, 32, n)
    amax = np.abs(w).max(1)
    if fmt == "e4m3":
        byte = np.frexp(amax)[1] - 1 + 127 - 7
    else:
        mant, ex = np.frexp(amax / 6.0)
        byte = np.where(mant > 0.5, ex, ex - 1) + 127
    byte = np.clip(np.where(amax > 0, byte, 1), 1, 254)
    scaled = (w * np.exp2(127.0 - byte)[:, None, :]).reshape(k, n).astype(np.float32)
    by_word = np.ascontiguousarray(scaled.reshape(k // 512, 128, 4, n).transpose(0, 1, 3, 2))
    if fmt == "e4m3":
        words = by_word.astype(ml_dtypes.float8_e4m3fn).view(np.uint8)
    else:
        c = by_word.astype(ml_dtypes.float4_e2m1fn).view(np.uint8) & 0xF
        words = c[..., 0::2] | (c[..., 1::2] << 4)
    return np.ascontiguousarray(words), np.ascontiguousarray(byte.astype(np.uint8).reshape(k // 512, 16, n))


def unpack_weight(words, scales, fmt):
    g, p, n, _ = words.shape
    if fmt == "e4m3":
        vals = np.ascontiguousarray(words).view(ml_dtypes.float8_e4m3fn).astype(np.float64)
    else:
        nib = np.empty((g, p, n, 4), np.uint8)
        nib[..., 0::2] = words & 0xF
        nib[..., 1::2] = words >> 4
        vals = E2M1[nib]
    vals = vals * np.repeat(np.exp2(scales.astype(np.float64) - 127.0), 8, axis=1)[..., None]
    return vals.transpose(0, 1, 3, 2).reshape(g * 512, n)


B, N_I, N_H1, N_H2, N_H3, N_H4 = 4096, 768, 256, 1024, 2048, 1024
K1 = N_I + N_H1
FMT = "e4m3"


def sigmoid(v):
    return 1.0 / (1.0 + np.exp(-v))


def setup_inputs():
    s = mx_kscale(K1)

    def w(gain):
        wide = np.random.standard_normal((N_H1, K1)) * gain / np.sqrt(K1) / s[None, :]
        return pack_weight(wide.T, FMT)

    def b():
        return bf(np.random.standard_normal(N_H1) * 0.3)

    X = bf(np.random.standard_normal((B, N_I)) * s[:N_I])
    hidden1 = bf(np.random.standard_normal((B, N_H1)) * s[N_I:])
    cell1 = bf(np.random.standard_normal((B, N_H1)))
    Wf1_words, Wf1_scales = w(1.0)
    bf1 = b()
    Wi1_words, Wi1_scales = w(1.0)
    bi1 = b()
    Wc1_words, Wc1_scales = w(5.0 / 3.0)
    bc1 = b()
    Wo1_words, Wo1_scales = w(1.0)
    bo1 = b()
    return {"X": X,
            "hidden1": hidden1,
            "cell1": cell1,
            "Wf1_words": Wf1_words, "Wf1_scales": Wf1_scales, "bf1": bf1,
            "Wi1_words": Wi1_words, "Wi1_scales": Wi1_scales, "bi1": bi1,
            "Wc1_words": Wc1_words, "Wc1_scales": Wc1_scales, "bc1": bc1,
            "Wo1_words": Wo1_words, "Wo1_scales": Wo1_scales, "bo1": bo1}


def reference(X, hidden1, cell1, Wf1_words, Wf1_scales, bf1, Wi1_words, Wi1_scales, bi1,
              Wc1_words, Wc1_scales, bc1, Wo1_words, Wo1_scales, bo1):
    zq = mxq(np.concatenate([f64(X), f64(hidden1)], axis=1), 1, "e4m3")
    f = sigmoid((zq @ unpack_weight(Wf1_words, Wf1_scales, FMT)) + f64(bf1))
    i = sigmoid((zq @ unpack_weight(Wi1_words, Wi1_scales, FMT)) + f64(bi1))
    cand = np.tanh((zq @ unpack_weight(Wc1_words, Wc1_scales, FMT)) + f64(bc1))
    o = sigmoid((zq @ unpack_weight(Wo1_words, Wo1_scales, FMT)) + f64(bo1))
    h_new = o * np.tanh(cand)
    c_new = f * f64(cell1) + cand * i
    return h_new, c_new

@@ -1,0 +1,263 @@
+from contextlib import ExitStack
+
+import concourse.masks as masks
+import concourse.mybir as mybir
+
+F32 = mybir.dt.float32
+BF16 = mybir.dt.bfloat16
+I32 = mybir.dt.int32
+U32 = mybir.dt.uint32
+U8 = mybir.dt.uint8
+FP8X4 = mybir.dt.float8_e4m3fn_x4
+ACT = mybir.ActivationFunctionType
+ALU = mybir.AluOpType
+
+P = 128
+BATCH, N_X, N_H = 4096, 768, 256
+K = N_X + N_H
+PACK = 4
+PASSES = K // (P * PACK)
+PASS_WORDS = P * PACK // 2
+HALVES = N_H // P
+ROW_TILES = BATCH // P
+UNIT_TILES = 2
+UNIT_ROWS = UNIT_TILES * P
+UNITS = ROW_TILES // UNIT_TILES
+FORGET, OUTPUT, INPUT, CAND = 0, 1, 2, 3
+QUADRANT = 32
+BLOCK_PARTITIONS = 8
+SCALE_ROWS = QUADRANT // BLOCK_PARTITIONS
+
+FLOPS = 2 * BATCH * K * 4 * N_H
+
+
+def tile_quest_pa_t_kernel(
+    tc, X, hidden1, cell1,
+    Wf1_words, Wf1_scales, bf1, Wi1_words, Wi1_scales, bi1,
+    Wc1_words, Wc1_scales, bc1, Wo1_words, Wo1_scales, bo1,
+    out_0, out_1,
+):
+    nc = tc.nc
+    x_rows = X.rearrange("(p t) k -> p t k", t=ROW_TILES)
+    hidden_rows = hidden1.rearrange("(p t) k -> p t k", t=ROW_TILES)
+    cell_rows = cell1.rearrange("(p t) n -> p t n", t=ROW_TILES)
+    h_rows = out_0.rearrange("(p t) n -> p t n", t=ROW_TILES)
+    c_rows = out_1.rearrange("(p t) n -> p t n", t=ROW_TILES)
+
+    with ExitStack() as ctx:
+        ctx.enter_context(tc.manual_schedule())
+        consts = ctx.enter_context(tc.tile_pool(name="consts", bufs=1))
+        resident = ctx.enter_context(tc.tile_pool(name="resident", bufs=UNITS))
+        work = ctx.enter_context(tc.tile_pool(name="work", bufs=2))
+        psum = ctx.enter_context(tc.psum_pool(name="psum", bufs=2))
+
+        z_sb, cell_sb, grouped, zq_words, zq_scales = {}, {}, {}, {}, {}
+        sig_t, pre, in_gate, cand, tanh_cand, back, h_new, c_new = {}, {}, {}, {}, {}, {}, {}, {}
+
+        def unit_tiles(u):
+            return slice(u * UNIT_TILES, (u + 1) * UNIT_TILES)
+
+        def load_z(u):
+            z_sb[u] = resident.tile([P, UNIT_TILES, K], BF16, name="z_sb")
+            nc.sync.dma_start(out=z_sb[u][:, :, 0:N_X], in_=x_rows[:, unit_tiles(u), :])
+            nc.sync.dma_start(out=z_sb[u][:, :, N_X:K], in_=hidden_rows[:, unit_tiles(u), :])
+
+        def load_cell(u):
+            cell_sb[u] = resident.tile([P, UNIT_TILES, N_H], BF16, name="cell_sb")
+            nc.sync.dma_start(out=cell_sb[u][:], in_=cell_rows[:, unit_tiles(u), :])
+
+        w_words = consts.tile([P, PASSES, 4, N_H], U32, align_bytes=64)
+        w_scales = consts.tile([P, PASSES, 4, N_H], U8, align_bytes=64)
+        nc.vector.memset(w_scales[:].rearrange("p g j n -> p (g j n)").bitcast(I32), 0)
+
+        def load_weight(gate, words, scales):
+            nc.sync.dma_start(
+                out=w_words[:, :, gate, :].bitcast(I32),
+                in_=words.rearrange("g p n t -> p g (n t)").bitcast(I32),
+            )
+            for r in range(SCALE_ROWS):
+                nc.sync.dma_start(
+                    out=w_scales[r:P:QUADRANT, :, gate, :].bitcast(I32),
+                    in_=scales[:, r : P // BLOCK_PARTITIONS : SCALE_ROWS, :]
+                    .rearrange("g q n -> q g n")
+                    .bitcast(I32),
+                )
+
+        ident = consts.tile([P, P], F32)
+        masks.make_identity(nc, ident[:])
+        ones = consts.tile([P, P], BF16)
+        nc.vector.memset(ones[:], 1.0)
+        bias_rows = consts.tile([P, P], F32)
+        nc.vector.memset(bias_rows[:], 0.0)
+        bias_first_row = consts.tile([P, 2 * N_H], BF16)
+        nc.vector.memset(bias_first_row[:], 0.0)
+        warm = consts.tile([P, 1], F32)
+        nc.vector.memset(warm[:], 0.0)
+        nc.scalar.activation(out=warm[:], in_=warm[:], func=ACT.Sigmoid)
+
+        load_z(0)
+        bias_fo = consts.tile([2 * HALVES, P], BF16)
+        nc.sync.dma_start(out=bias_fo[0:HALVES, :], in_=bf1.rearrange("(h n) -> h n", h=HALVES))
+        nc.sync.dma_start(
+            out=bias_fo[HALVES : 2 * HALVES, :], in_=bo1.rearrange("(h n) -> h n", h=HALVES)
+        )
+        bias_ic = consts.tile([1, 2 * N_H], BF16)
+        nc.sync.dma_start(out=bias_ic[:, 0:N_H], in_=bi1.rearrange("(o n) -> o n", o=1))
+        nc.sync.dma_start(out=bias_ic[:, N_H : 2 * N_H], in_=bc1.rearrange("(o n) -> o n", o=1))
+        load_z(1)
+        load_weight(FORGET, Wf1_words, Wf1_scales)
+        load_weight(OUTPUT, Wo1_words, Wo1_scales)
+        load_weight(INPUT, Wi1_words, Wi1_scales)
+        load_weight(CAND, Wc1_words, Wc1_scales)
+        load_cell(0)
+        for u in range(2, UNITS):
+            load_z(u)
+            load_cell(u - 1)
+        load_cell(UNITS - 1)
+
+        bias_col = consts.tile([P, 2 * HALVES], F32)
+        bias_all_rows = consts.tile([P, 2 * N_H], F32)
+
+        def prepare_biases():
+            nc.vector.tensor_copy(out=bias_rows[0 : 2 * HALVES, :], in_=bias_fo[:])
+            bias_t = psum.tile([P, P], F32, tag="back")
+            nc.tensor.transpose(bias_t[:], bias_rows[:], ident[:])
+            nc.vector.tensor_copy(out=bias_col[:], in_=bias_t[:, 0 : 2 * HALVES])
+            nc.vector.tensor_copy(out=bias_first_row[0:1, :], in_=bias_ic[:])
+            bias_sum = psum.tile([P, 2 * N_H], F32, tag="back")
+            nc.tensor.matmul(
+                out=bias_sum[:], lhsT=ones[:], rhs=bias_first_row[:], start=True, stop=True
+            )
+            nc.vector.tensor_copy(out=bias_all_rows[:], in_=bias_sum[:])
+
+        def transpose_z(u):
+            grouped[u] = work.tile(
+                [P, PASSES, UNIT_ROWS, PACK], BF16, name="grouped", align_bytes=64
+            )
+            for r in range(UNIT_TILES):
+                words = z_sb[u][:, r, :].bitcast(F32)
+                z_t = psum.tile([P, PASSES, 2, P], F32, name="z_t")
+                for g in range(PASSES):
+                    for pair in range(2):
+                        nc.tensor.transpose(
+                            z_t[:, g, pair, :],
+                            words[:, g * PASS_WORDS + pair : (g + 1) * PASS_WORDS : 2],
+                            ident[:],
+                        )
+                copy_out = nc.scalar.copy if r % 2 == 0 else nc.vector.tensor_copy
+                copy_out(
+                    out=grouped[u][:, :, r * P : (r + 1) * P, :].bitcast(F32),
+                    in_=z_t[:].rearrange("p g pair r -> p g r pair"),
+                )
+
+        def quantise_z(u):
+            zq_words[u] = work.tile([P, PASSES, UNIT_ROWS], U32, name="zq_words", align_bytes=64)
+            zq_scales[u] = work.tile([P, PASSES, UNIT_ROWS], U8, name="zq_scales", align_bytes=64)
+            nc.vector.quantize_mx(
+                out=zq_words[u][:].rearrange("p g r -> p (g r)").bitcast(FP8X4),
+                scales=zq_scales[u][:].rearrange("p g r -> p (g r)"),
+                in_=grouped[u][:].rearrange("p g r t -> p (g r t)"),
+            )
+
+        def gates_with_features_on_partitions(u):
+            sig_t[u] = work.tile([P, 2, HALVES, UNIT_ROWS], F32, name="sig_t")
+            for gate in (FORGET, OUTPUT):
+                acc = psum.tile([P, HALVES, UNIT_ROWS], F32, name="acc_features")
+                for h in range(HALVES):
+                    features = slice(h * P, (h + 1) * P)
+                    for g in range(PASSES):
+                        nc.tensor.matmul_mx(
+                            out=acc[:, h, :],
+                            lhsT=w_words[:, g, gate, features].bitcast(FP8X4),
+                            lhsT_scale=w_scales[:, g, gate, features],
+                            rhs=zq_words[u][:, g, :].bitcast(FP8X4),
+                            rhs_scale=zq_scales[u][:, g, :],
+                            start=(g == 0),
+                            stop=(g == PASSES - 1),
+                        )
+                for h in range(HALVES):
+                    column = gate * HALVES + h
+                    nc.scalar.activation(
+                        out=sig_t[u][:, gate, h, :],
+                        in_=acc[:, h, :],
+                        func=ACT.Sigmoid,
+                        bias=bias_col[:, column : column + 1],
+                    )
+
+        def gates_with_rows_on_partitions(u):
+            pre[u] = work.tile([P, UNIT_TILES, 2 * N_H], F32, name="pre")
+            for r in range(UNIT_TILES):
+                rows = slice(r * P, (r + 1) * P)
+                acc = psum.tile([P, 2 * N_H], F32, name="acc_rows")
+                for g in range(PASSES):
+                    nc.tensor.matmul_mx(
+                        out=acc[:],
+                        lhsT=zq_words[u][:, g, rows].bitcast(FP8X4),
+                        lhsT_scale=zq_scales[u][:, g, rows],
+                        rhs=w_words[:, g, INPUT : CAND + 1, :]
+                        .rearrange("p j n -> p (j n)")
+                        .bitcast(FP8X4),
+                        rhs_scale=w_scales[:, g, INPUT : CAND + 1, :].rearrange("p j n -> p (j n)"),
+                        start=(g == 0),
+                        stop=(g == PASSES - 1),
+                    )
+                nc.vector.tensor_tensor(
+                    out=pre[u][:, r, :], in0=acc[:], in1=bias_all_rows[:], op=ALU.add
+                )
+
+        def activate_rows(u):
+            in_gate[u] = work.tile([P, UNIT_TILES, N_H], F32, name="in_gate")
+            cand[u] = work.tile([P, UNIT_TILES, N_H], F32, name="cand")
+            tanh_cand[u] = work.tile([P, UNIT_TILES, N_H], F32, name="tanh_cand")
+            nc.scalar.activation(out=in_gate[u][:], in_=pre[u][:, :, 0:N_H], func=ACT.Sigmoid)
+            nc.scalar.activation(out=cand[u][:], in_=pre[u][:, :, N_H : 2 * N_H], func=ACT.Tanh)
+            nc.scalar.activation(out=tanh_cand[u][:], in_=cand[u][:], func=ACT.Tanh)
+            nc.gpsimd.tensor_tensor(out=in_gate[u][:], in0=in_gate[u][:], in1=cand[u][:], op=ALU.mult)
+
+        def transpose_back(u):
+            c_new[u] = resident.tile([P, UNIT_TILES, N_H], F32, name="c_new")
+            for r in range(UNIT_TILES):
+                back[u, r] = psum.tile([P, 2, HALVES, P], F32, name="back")
+                for gate in (FORGET, OUTPUT):
+                    for h in range(HALVES):
+                        nc.tensor.transpose(
+                            back[u, r][:, gate, h, :],
+                            sig_t[u][:, gate, h, r * P : (r + 1) * P],
+                            ident[:],
+                        )
+                nc.vector.tensor_tensor(
+                    out=c_new[u][:, r, :],
+                    in0=back[u, r][:, FORGET, :, :].rearrange("p h n -> p (h n)"),
+                    in1=cell_sb[u][:, r, :],
+                    op=ALU.mult,
+                )
+
+        def finish(u):
+            h_new[u] = resident.tile([P, UNIT_TILES, N_H], F32, name="h_new")
+            for r in range(UNIT_TILES):
+                nc.vector.tensor_tensor(
+                    out=h_new[u][:, r, :],
+                    in0=back[u, r][:, OUTPUT, :, :].rearrange("p h n -> p (h n)"),
+                    in1=tanh_cand[u][:, r, :],
+                    op=ALU.mult,
+                )
+            nc.sync.dma_start(out=h_rows[:, unit_tiles(u), :], in_=h_new[u][:])
+            nc.gpsimd.tensor_tensor(out=c_new[u][:], in0=c_new[u][:], in1=in_gate[u][:], op=ALU.add)
+            nc.sync.dma_start(out=c_rows[:, unit_tiles(u), :], in_=c_new[u][:])
+
+        transpose_z(0)
+        prepare_biases()
+        quantise_z(0)
+        for n in range(UNITS + 1):
+            if n + 1 < UNITS:
+                transpose_z(n + 1)
+            if n >= 1:
+                activate_rows(n - 1)
+                transpose_back(n - 1)
+            if n + 1 < UNITS:
+                quantise_z(n + 1)
+            if n >= 1:
+                finish(n - 1)
+            if n < UNITS:
+                gates_with_features_on_partitions(n)
+                gates_with_rows_on_partitions(n)

@@ -52,7 +52,7 @@ def tile_quest_pa_t_kernel(
         psum = ctx.enter_context(tc.psum_pool(name="psum", bufs=2))
 
         z_sb, cell_sb, grouped, zq_words, zq_scales = {}, {}, {}, {}, {}
-        sig_t, pre, in_gate, cand, tanh_cand, back, h_new, c_new = {}, {}, {}, {}, {}, {}, {}, {}
+        sig_t, pre, in_gate, cand, tanh_cand, h_new, c_new = {}, {}, {}, {}, {}, {}, {}
 
         def unit_tiles(u):
             return slice(u * UNIT_TILES, (u + 1) * UNIT_TILES)
@@ -71,9 +71,9 @@ def tile_quest_pa_t_kernel(
         nc.vector.memset(w_scales[:].rearrange("p g j n -> p (g j n)").bitcast(I32), 0)
 
         def load_weight(gate, words, scales):
-            nc.sync.dma_start(
-                out=w_words[:, :, gate, :].bitcast(I32),
-                in_=words.rearrange("g p n t -> p g (n t)").bitcast(I32),
+            nc.gpsimd.dma_start(
+                out=w_words[:, :, gate, :].bitcast(F32),
+                in_=words.rearrange("g p n t -> p g (n t)").bitcast(F32),
             )
             for r in range(SCALE_ROWS):
                 nc.sync.dma_start(
@@ -205,44 +205,43 @@ def tile_quest_pa_t_kernel(
                     out=pre[u][:, r, :], in0=acc[:], in1=bias_all_rows[:], op=ALU.add
                 )
 
-        def activate_rows(u):
-            in_gate[u] = work.tile([P, UNIT_TILES, N_H], F32, name="in_gate")
-            cand[u] = work.tile([P, UNIT_TILES, N_H], F32, name="cand")
-            tanh_cand[u] = work.tile([P, UNIT_TILES, N_H], F32, name="tanh_cand")
-            nc.scalar.activation(out=in_gate[u][:], in_=pre[u][:, :, 0:N_H], func=ACT.Sigmoid)
-            nc.scalar.activation(out=cand[u][:], in_=pre[u][:, :, N_H : 2 * N_H], func=ACT.Tanh)
-            nc.scalar.activation(out=tanh_cand[u][:], in_=cand[u][:], func=ACT.Tanh)
-            nc.gpsimd.tensor_tensor(out=in_gate[u][:], in0=in_gate[u][:], in1=cand[u][:], op=ALU.mult)
+        def finish_row_tile(u, r):
+            if r == 0:
+                in_gate[u] = work.tile([P, UNIT_TILES, N_H], F32, name="in_gate")
+                cand[u] = work.tile([P, UNIT_TILES, N_H], F32, name="cand")
+                tanh_cand[u] = work.tile([P, UNIT_TILES, N_H], F32, name="tanh_cand")
+                h_new[u] = resident.tile([P, UNIT_TILES, N_H], F32, name="h_new")
+                c_new[u] = resident.tile([P, UNIT_TILES, N_H], F32, name="c_new")
+            nc.scalar.activation(out=cand[u][:, r, :], in_=pre[u][:, r, N_H : 2 * N_H], func=ACT.Tanh)
+            nc.scalar.activation(out=in_gate[u][:, r, :], in_=pre[u][:, r, 0:N_H], func=ACT.Sigmoid)
+            nc.gpsimd.tensor_tensor(
+                out=in_gate[u][:, r, :], in0=in_gate[u][:, r, :], in1=cand[u][:, r, :], op=ALU.mult
+            )
+            nc.scalar.activation(out=tanh_cand[u][:, r, :], in_=cand[u][:, r, :], func=ACT.Tanh)
+            back = psum.tile([P, 2, HALVES, P], F32, name="back")
+            for gate in (FORGET, OUTPUT):
+                for h in range(HALVES):
+                    nc.tensor.transpose(
+                        back[:, gate, h, :], sig_t[u][:, gate, h, r * P : (r + 1) * P], ident[:]
+                    )
+            nc.vector.tensor_tensor(
+                out=c_new[u][:, r, :],
+                in0=back[:, FORGET, :, :].rearrange("p h n -> p (h n)"),
+                in1=cell_sb[u][:, r, :],
+                op=ALU.mult,
+            )
+            nc.vector.tensor_tensor(
+                out=h_new[u][:, r, :],
+                in0=back[:, OUTPUT, :, :].rearrange("p h n -> p (h n)"),
+                in1=tanh_cand[u][:, r, :],
+                op=ALU.mult,
+            )
+            nc.gpsimd.tensor_tensor(
+                out=c_new[u][:, r, :], in0=c_new[u][:, r, :], in1=in_gate[u][:, r, :], op=ALU.add
+            )
 
-        def transpose_back(u):
-            c_new[u] = resident.tile([P, UNIT_TILES, N_H], F32, name="c_new")
-            for r in range(UNIT_TILES):
-                back[u, r] = psum.tile([P, 2, HALVES, P], F32, name="back")
-                for gate in (FORGET, OUTPUT):
-                    for h in range(HALVES):
-                        nc.tensor.transpose(
-                            back[u, r][:, gate, h, :],
-                            sig_t[u][:, gate, h, r * P : (r + 1) * P],
-                            ident[:],
-                        )
-                nc.vector.tensor_tensor(
-                    out=c_new[u][:, r, :],
-                    in0=back[u, r][:, FORGET, :, :].rearrange("p h n -> p (h n)"),
-                    in1=cell_sb[u][:, r, :],
-                    op=ALU.mult,
-                )
-
-        def finish(u):
-            h_new[u] = resident.tile([P, UNIT_TILES, N_H], F32, name="h_new")
-            for r in range(UNIT_TILES):
-                nc.vector.tensor_tensor(
-                    out=h_new[u][:, r, :],
-                    in0=back[u, r][:, OUTPUT, :, :].rearrange("p h n -> p (h n)"),
-                    in1=tanh_cand[u][:, r, :],
-                    op=ALU.mult,
-                )
+        def store(u):
             nc.sync.dma_start(out=h_rows[:, unit_tiles(u), :], in_=h_new[u][:])
-            nc.gpsimd.tensor_tensor(out=c_new[u][:], in0=c_new[u][:], in1=in_gate[u][:], op=ALU.add)
             nc.sync.dma_start(out=c_rows[:, unit_tiles(u), :], in_=c_new[u][:])
 
         transpose_z(0)
@@ -252,12 +251,12 @@ def tile_quest_pa_t_kernel(
             if n + 1 < UNITS:
                 transpose_z(n + 1)
             if n >= 1:
-                activate_rows(n - 1)
-                transpose_back(n - 1)
+                finish_row_tile(n - 1, 0)
             if n + 1 < UNITS:
                 quantise_z(n + 1)
             if n >= 1:
-                finish(n - 1)
+                finish_row_tile(n - 1, 1)
+                store(n - 1)
             if n < UNITS:
                 gates_with_features_on_partitions(n)
                 gates_with_rows_on_partitions(n)

@@ -71,9 +71,9 @@ def tile_quest_pa_t_kernel(
         nc.vector.memset(w_scales[:].rearrange("p g j n -> p (g j n)").bitcast(I32), 0)
 
         def load_weight(gate, words, scales):
-            nc.gpsimd.dma_start(
-                out=w_words[:, :, gate, :].bitcast(F32),
-                in_=words.rearrange("g p n t -> p g (n t)").bitcast(F32),
+            nc.sync.dma_start(
+                out=w_words[:, :, gate, :].bitcast(I32),
+                in_=words.rearrange("g p n t -> p g (n t)").bitcast(I32),
             )
             for r in range(SCALE_ROWS):
                 nc.sync.dma_start(

@@ -214,7 +214,8 @@ def tile_quest_pa_t_kernel(
                 c_new[u] = resident.tile([P, UNIT_TILES, N_H], F32, name="c_new")
             nc.scalar.activation(out=cand[u][:, r, :], in_=pre[u][:, r, N_H : 2 * N_H], func=ACT.Tanh)
             nc.scalar.activation(out=in_gate[u][:, r, :], in_=pre[u][:, r, 0:N_H], func=ACT.Sigmoid)
-            nc.gpsimd.tensor_tensor(
+            helper = nc.vector if u == UNITS - 1 else nc.gpsimd
+            helper.tensor_tensor(
                 out=in_gate[u][:, r, :], in0=in_gate[u][:, r, :], in1=cand[u][:, r, :], op=ALU.mult
             )
             nc.scalar.activation(out=tanh_cand[u][:, r, :], in_=cand[u][:, r, :], func=ACT.Tanh)
@@ -230,15 +231,19 @@ def tile_quest_pa_t_kernel(
                 in1=cell_sb[u][:, r, :],
                 op=ALU.mult,
             )
+            helper.tensor_tensor(
+                out=c_new[u][:, r, :], in0=c_new[u][:, r, :], in1=in_gate[u][:, r, :], op=ALU.add
+            )
+            if u == UNITS - 1:
+                nc.sync.dma_start(out=c_rows[:, u * UNIT_TILES + r, :], in_=c_new[u][:, r, :])
             nc.vector.tensor_tensor(
                 out=h_new[u][:, r, :],
                 in0=back[:, OUTPUT, :, :].rearrange("p h n -> p (h n)"),
                 in1=tanh_cand[u][:, r, :],
                 op=ALU.mult,
             )
-            nc.gpsimd.tensor_tensor(
-                out=c_new[u][:, r, :], in0=c_new[u][:, r, :], in1=in_gate[u][:, r, :], op=ALU.add
-            )
+            if u == UNITS - 1:
+                nc.sync.dma_start(out=h_rows[:, u * UNIT_TILES + r, :], in_=h_new[u][:, r, :])
 
         def store(u):
             nc.sync.dma_start(out=h_rows[:, unit_tiles(u), :], in_=h_new[u][:])
@@ -256,6 +261,7 @@ def tile_quest_pa_t_kernel(
                 quantise_z(n + 1)
             if n >= 1:
                 finish_row_tile(n - 1, 1)
+            if 1 <= n < UNITS:
                 store(n - 1)
             if n < UNITS:
                 gates_with_features_on_partitions(n)

@@ -95,24 +95,24 @@ def tile_quest_pa_t_kernel(
         nc.vector.memset(warm[:], 0.0)
         nc.scalar.activation(out=warm[:], in_=warm[:], func=ACT.Sigmoid)
 
-        load_z(0)
         bias_fo = consts.tile([2 * HALVES, P], BF16)
-        nc.sync.dma_start(out=bias_fo[0:HALVES, :], in_=bf1.rearrange("(h n) -> h n", h=HALVES))
-        nc.sync.dma_start(
+        nc.gpsimd.dma_start(out=bias_fo[0:HALVES, :], in_=bf1.rearrange("(h n) -> h n", h=HALVES))
+        nc.gpsimd.dma_start(
             out=bias_fo[HALVES : 2 * HALVES, :], in_=bo1.rearrange("(h n) -> h n", h=HALVES)
         )
         bias_ic = consts.tile([1, 2 * N_H], BF16)
-        nc.sync.dma_start(out=bias_ic[:, 0:N_H], in_=bi1.rearrange("(o n) -> o n", o=1))
-        nc.sync.dma_start(out=bias_ic[:, N_H : 2 * N_H], in_=bc1.rearrange("(o n) -> o n", o=1))
+        nc.gpsimd.dma_start(out=bias_ic[:, 0:N_H], in_=bi1.rearrange("(o n) -> o n", o=1))
+        nc.gpsimd.dma_start(out=bias_ic[:, N_H : 2 * N_H], in_=bc1.rearrange("(o n) -> o n", o=1))
+        load_z(0)
         load_z(1)
         load_weight(FORGET, Wf1_words, Wf1_scales)
         load_weight(OUTPUT, Wo1_words, Wo1_scales)
         load_weight(INPUT, Wi1_words, Wi1_scales)
         load_weight(CAND, Wc1_words, Wc1_scales)
-        load_cell(0)
         for u in range(2, UNITS):
             load_z(u)
-            load_cell(u - 1)
+            load_cell(u - 2)
+        load_cell(UNITS - 2)
         load_cell(UNITS - 1)
 
         bias_col = consts.tile([P, 2 * HALVES], F32)
@@ -159,30 +159,44 @@ def tile_quest_pa_t_kernel(
                 in_=grouped[u][:].rearrange("p g r t -> p (g r t)"),
             )
 
+        def multiply_features_on_partitions(u, gate):
+            acc = psum.tile([P, HALVES, UNIT_ROWS], F32, name="acc_features")
+            for h in range(HALVES):
+                features = slice(h * P, (h + 1) * P)
+                for g in range(PASSES):
+                    nc.tensor.matmul_mx(
+                        out=acc[:, h, :],
+                        lhsT=w_words[:, g, gate, features].bitcast(FP8X4),
+                        lhsT_scale=w_scales[:, g, gate, features],
+                        rhs=zq_words[u][:, g, :].bitcast(FP8X4),
+                        rhs_scale=zq_scales[u][:, g, :],
+                        start=(g == 0),
+                        stop=(g == PASSES - 1),
+                    )
+            return acc
+
+        def sigmoid_features_on_partitions(u, gate, acc):
+            for h in range(HALVES):
+                column = gate * HALVES + h
+                nc.scalar.activation(
+                    out=sig_t[u][:, gate, h, :],
+                    in_=acc[:, h, :],
+                    func=ACT.Sigmoid,
+                    bias=bias_col[:, column : column + 1],
+                )
+
         def gates_with_features_on_partitions(u):
             sig_t[u] = work.tile([P, 2, HALVES, UNIT_ROWS], F32, name="sig_t")
-            for gate in (FORGET, OUTPUT):
-                acc = psum.tile([P, HALVES, UNIT_ROWS], F32, name="acc_features")
-                for h in range(HALVES):
-                    features = slice(h * P, (h + 1) * P)
-                    for g in range(PASSES):
-                        nc.tensor.matmul_mx(
-                            out=acc[:, h, :],
-                            lhsT=w_words[:, g, gate, features].bitcast(FP8X4),
-                            lhsT_scale=w_scales[:, g, gate, features],
-                            rhs=zq_words[u][:, g, :].bitcast(FP8X4),
-                            rhs_scale=zq_scales[u][:, g, :],
-                            start=(g == 0),
-                            stop=(g == PASSES - 1),
-                        )
-                for h in range(HALVES):
-                    column = gate * HALVES + h
-                    nc.scalar.activation(
-                        out=sig_t[u][:, gate, h, :],
-                        in_=acc[:, h, :],
-                        func=ACT.Sigmoid,
-                        bias=bias_col[:, column : column + 1],
-                    )
+            if u == 0:
+                acc_forget = multiply_features_on_partitions(u, FORGET)
+                acc_output = multiply_features_on_partitions(u, OUTPUT)
+                prepare_biases()
+                sigmoid_features_on_partitions(u, FORGET, acc_forget)
+                sigmoid_features_on_partitions(u, OUTPUT, acc_output)
+            else:
+                for gate in (FORGET, OUTPUT):
+                    acc = multiply_features_on_partitions(u, gate)
+                    sigmoid_features_on_partitions(u, gate, acc)
 
         def gates_with_rows_on_partitions(u):
             pre[u] = work.tile([P, UNIT_TILES, 2 * N_H], F32, name="pre")
@@ -250,7 +264,6 @@ def tile_quest_pa_t_kernel(
             nc.sync.dma_start(out=c_rows[:, unit_tiles(u), :], in_=c_new[u][:])
 
         transpose_z(0)
-        prepare_biases()
         quantise_z(0)
         for n in range(UNITS + 1):
             if n + 1 < UNITS:

@@ -27,6 +27,8 @@ FORGET, OUTPUT, INPUT, CAND = 0, 1, 2, 3
 QUADRANT = 32
 BLOCK_PARTITIONS = 8
 SCALE_ROWS = QUADRANT // BLOCK_PARTITIONS
+WARM_UP_MATMULS = 9
+BRIDGE_MATMULS = 3
 
 FLOPS = 2 * BATCH * K * 4 * N_H
 
@@ -66,6 +68,18 @@ def tile_quest_pa_t_kernel(
             cell_sb[u] = resident.tile([P, UNIT_TILES, N_H], BF16, name="cell_sb")
             nc.sync.dma_start(out=cell_sb[u][:], in_=cell_rows[:, unit_tiles(u), :])
 
+        ones = consts.tile([P, 2 * P], BF16)
+        nc.vector.memset(ones[:], 1.0)
+
+        def keep_clock_up(matmuls):
+            idle_product = psum.tile([P, 2 * P], F32, tag="back")
+            for i in range(matmuls):
+                nc.tensor.matmul(
+                    out=idle_product[:], lhsT=ones[:, 0:P], rhs=ones[:], start=True, stop=True
+                )
+
+        keep_clock_up(WARM_UP_MATMULS)
+
         w_words = consts.tile([P, PASSES, 4, N_H], U32, align_bytes=64)
         w_scales = consts.tile([P, PASSES, 4, N_H], U8, align_bytes=64)
         nc.vector.memset(w_scales[:].rearrange("p g j n -> p (g j n)").bitcast(I32), 0)
@@ -85,8 +99,6 @@ def tile_quest_pa_t_kernel(
 
         ident = consts.tile([P, P], F32)
         masks.make_identity(nc, ident[:])
-        ones = consts.tile([P, P], BF16)
-        nc.vector.memset(ones[:], 1.0)
         bias_rows = consts.tile([P, P], F32)
         nc.vector.memset(bias_rows[:], 0.0)
         bias_first_row = consts.tile([P, 2 * N_H], BF16)
@@ -126,7 +138,7 @@ def tile_quest_pa_t_kernel(
             nc.vector.tensor_copy(out=bias_first_row[0:1, :], in_=bias_ic[:])
             bias_sum = psum.tile([P, 2 * N_H], F32, tag="back")
             nc.tensor.matmul(
-                out=bias_sum[:], lhsT=ones[:], rhs=bias_first_row[:], start=True, stop=True
+                out=bias_sum[:], lhsT=ones[:, 0:P], rhs=bias_first_row[:], start=True, stop=True
             )
             nc.vector.tensor_copy(out=bias_all_rows[:], in_=bias_sum[:])
 
@@ -265,9 +277,12 @@ def tile_quest_pa_t_kernel(
 
         transpose_z(0)
         quantise_z(0)
+        keep_clock_up(BRIDGE_MATMULS)
         for n in range(UNITS + 1):
             if n + 1 < UNITS:
                 transpose_z(n + 1)
+            if n == 0:
+                keep_clock_up(BRIDGE_MATMULS)
             if n >= 1:
                 finish_row_tile(n - 1, 0)
             if n + 1 < UNITS:

@@ -240,7 +240,7 @@ def tile_quest_pa_t_kernel(
                 c_new[u] = resident.tile([P, UNIT_TILES, N_H], F32, name="c_new")
             nc.scalar.activation(out=cand[u][:, r, :], in_=pre[u][:, r, N_H : 2 * N_H], func=ACT.Tanh)
             nc.scalar.activation(out=in_gate[u][:, r, :], in_=pre[u][:, r, 0:N_H], func=ACT.Sigmoid)
-            helper = nc.vector if u == UNITS - 1 else nc.gpsimd
+            helper = nc.vector if u == UNITS - 1 and r == UNIT_TILES - 1 else nc.gpsimd
             helper.tensor_tensor(
                 out=in_gate[u][:, r, :], in0=in_gate[u][:, r, :], in1=cand[u][:, r, :], op=ALU.mult
             )

@@ -227,9 +227,17 @@ def tile_quest_pa_t_kernel(
                         start=(g == 0),
                         stop=(g == PASSES - 1),
                     )
-                nc.vector.tensor_tensor(
-                    out=pre[u][:, r, :], in0=acc[:], in1=bias_all_rows[:], op=ALU.add
-                )
+                if u == UNITS - 1:
+                    halves = (slice(N_H, 2 * N_H), slice(0, N_H))
+                else:
+                    halves = (slice(0, 2 * N_H),)
+                for columns in halves:
+                    nc.vector.tensor_tensor(
+                        out=pre[u][:, r, columns],
+                        in0=acc[:, columns],
+                        in1=bias_all_rows[:, columns],
+                        op=ALU.add,
+                    )
 
         def finish_row_tile(u, r):
             if r == 0:
@@ -238,13 +246,9 @@ def tile_quest_pa_t_kernel(
                 tanh_cand[u] = work.tile([P, UNIT_TILES, N_H], F32, name="tanh_cand")
                 h_new[u] = resident.tile([P, UNIT_TILES, N_H], F32, name="h_new")
                 c_new[u] = resident.tile([P, UNIT_TILES, N_H], F32, name="c_new")
+            last_unit = u == UNITS - 1
+            last_tile = last_unit and r == UNIT_TILES - 1
             nc.scalar.activation(out=cand[u][:, r, :], in_=pre[u][:, r, N_H : 2 * N_H], func=ACT.Tanh)
-            nc.scalar.activation(out=in_gate[u][:, r, :], in_=pre[u][:, r, 0:N_H], func=ACT.Sigmoid)
-            helper = nc.vector if u == UNITS - 1 and r == UNIT_TILES - 1 else nc.gpsimd
-            helper.tensor_tensor(
-                out=in_gate[u][:, r, :], in0=in_gate[u][:, r, :], in1=cand[u][:, r, :], op=ALU.mult
-            )
-            nc.scalar.activation(out=tanh_cand[u][:, r, :], in_=cand[u][:, r, :], func=ACT.Tanh)
             back = psum.tile([P, 2, HALVES, P], F32, name="back")
             for gate in (FORGET, OUTPUT):
                 for h in range(HALVES):
@@ -257,19 +261,41 @@ def tile_quest_pa_t_kernel(
                 in1=cell_sb[u][:, r, :],
                 op=ALU.mult,
             )
-            helper.tensor_tensor(
-                out=c_new[u][:, r, :], in0=c_new[u][:, r, :], in1=in_gate[u][:, r, :], op=ALU.add
-            )
-            if u == UNITS - 1:
-                nc.sync.dma_start(out=c_rows[:, u * UNIT_TILES + r, :], in_=c_new[u][:, r, :])
-            nc.vector.tensor_tensor(
-                out=h_new[u][:, r, :],
-                in0=back[:, OUTPUT, :, :].rearrange("p h n -> p (h n)"),
-                in1=tanh_cand[u][:, r, :],
-                op=ALU.mult,
-            )
-            if u == UNITS - 1:
-                nc.sync.dma_start(out=h_rows[:, u * UNIT_TILES + r, :], in_=h_new[u][:, r, :])
+
+            def input_gate_times_candidate(engine):
+                nc.scalar.activation(
+                    out=in_gate[u][:, r, :], in_=pre[u][:, r, 0:N_H], func=ACT.Sigmoid
+                )
+                engine.tensor_tensor(
+                    out=in_gate[u][:, r, :], in0=in_gate[u][:, r, :], in1=cand[u][:, r, :], op=ALU.mult
+                )
+
+            def sum_for_c_new(engine):
+                engine.tensor_tensor(
+                    out=c_new[u][:, r, :], in0=c_new[u][:, r, :], in1=in_gate[u][:, r, :], op=ALU.add
+                )
+                if last_unit:
+                    nc.sync.dma_start(out=c_rows[:, u * UNIT_TILES + r, :], in_=c_new[u][:, r, :])
+
+            def output_gate_times_tanh():
+                nc.scalar.activation(out=tanh_cand[u][:, r, :], in_=cand[u][:, r, :], func=ACT.Tanh)
+                nc.vector.tensor_tensor(
+                    out=h_new[u][:, r, :],
+                    in0=back[:, OUTPUT, :, :].rearrange("p h n -> p (h n)"),
+                    in1=tanh_cand[u][:, r, :],
+                    op=ALU.mult,
+                )
+                if last_unit:
+                    nc.sync.dma_start(out=h_rows[:, u * UNIT_TILES + r, :], in_=h_new[u][:, r, :])
+
+            helper = nc.vector if last_tile else nc.gpsimd
+            input_gate_times_candidate(helper)
+            if last_unit:
+                output_gate_times_tanh()
+                sum_for_c_new(helper)
+            else:
+                sum_for_c_new(helper)
+                output_gate_times_tanh()
 
         def store(u):
             nc.sync.dma_start(out=h_rows[:, unit_tiles(u), :], in_=h_new[u][:])

@@ -27,8 +27,6 @@ FORGET, OUTPUT, INPUT, CAND = 0, 1, 2, 3
 QUADRANT = 32
 BLOCK_PARTITIONS = 8
 SCALE_ROWS = QUADRANT // BLOCK_PARTITIONS
-WARM_UP_MATMULS = 9
-BRIDGE_MATMULS = 3
 
 FLOPS = 2 * BATCH * K * 4 * N_H
 
@@ -70,15 +68,6 @@ def tile_quest_pa_t_kernel(
 
         ones = consts.tile([P, 2 * P], BF16)
         nc.vector.memset(ones[:], 1.0)
-
-        def keep_clock_up(matmuls):
-            idle_product = psum.tile([P, 2 * P], F32, tag="back")
-            for i in range(matmuls):
-                nc.tensor.matmul(
-                    out=idle_product[:], lhsT=ones[:, 0:P], rhs=ones[:], start=True, stop=True
-                )
-
-        keep_clock_up(WARM_UP_MATMULS)
 
         w_words = consts.tile([P, PASSES, 4, N_H], U32, align_bytes=64)
         w_scales = consts.tile([P, PASSES, 4, N_H], U8, align_bytes=64)
@@ -303,12 +292,9 @@ def tile_quest_pa_t_kernel(
 
         transpose_z(0)
         quantise_z(0)
-        keep_clock_up(BRIDGE_MATMULS)
         for n in range(UNITS + 1):
             if n + 1 < UNITS:
                 transpose_z(n + 1)
-            if n == 0:
-                keep_clock_up(BRIDGE_MATMULS)
             if n >= 1:
                 finish_row_tile(n - 1, 0)
             if n + 1 < UNITS:

from contextlib import ExitStack

import concourse.masks as masks
import concourse.mybir as mybir

F32 = mybir.dt.float32
BF16 = mybir.dt.bfloat16
I32 = mybir.dt.int32
U32 = mybir.dt.uint32
U8 = mybir.dt.uint8
FP8X4 = mybir.dt.float8_e4m3fn_x4
ACT = mybir.ActivationFunctionType
ALU = mybir.AluOpType

P = 128
BATCH, N_X, N_H = 4096, 768, 256
K = N_X + N_H
PACK = 4
PASSES = K // (P * PACK)
PASS_WORDS = P * PACK // 2
HALVES = N_H // P
ROW_TILES = BATCH // P
UNIT_TILES = 2
UNIT_ROWS = UNIT_TILES * P
UNITS = ROW_TILES // UNIT_TILES
FORGET, OUTPUT, INPUT, CAND = 0, 1, 2, 3
QUADRANT = 32
BLOCK_PARTITIONS = 8
SCALE_ROWS = QUADRANT // BLOCK_PARTITIONS

FLOPS = 2 * BATCH * K * 4 * N_H


def tile_quest_pa_t_kernel(
    tc, X, hidden1, cell1,
    Wf1_words, Wf1_scales, bf1, Wi1_words, Wi1_scales, bi1,
    Wc1_words, Wc1_scales, bc1, Wo1_words, Wo1_scales, bo1,
    out_0, out_1,
):
    nc = tc.nc
    x_rows = X.rearrange("(p t) k -> p t k", t=ROW_TILES)
    hidden_rows = hidden1.rearrange("(p t) k -> p t k", t=ROW_TILES)
    cell_rows = cell1.rearrange("(p t) n -> p t n", t=ROW_TILES)
    h_rows = out_0.rearrange("(p t) n -> p t n", t=ROW_TILES)
    c_rows = out_1.rearrange("(p t) n -> p t n", t=ROW_TILES)

    with ExitStack() as ctx:
        ctx.enter_context(tc.manual_schedule())
        consts = ctx.enter_context(tc.tile_pool(name="consts", bufs=1))
        resident = ctx.enter_context(tc.tile_pool(name="resident", bufs=UNITS))
        work = ctx.enter_context(tc.tile_pool(name="work", bufs=2))
        psum = ctx.enter_context(tc.psum_pool(name="psum", bufs=2))

        z_sb, cell_sb, grouped, zq_words, zq_scales = {}, {}, {}, {}, {}
        sig_t, pre, in_gate, cand, tanh_cand, h_new, c_new = {}, {}, {}, {}, {}, {}, {}

        def unit_tiles(u):
            return slice(u * UNIT_TILES, (u + 1) * UNIT_TILES)

        def load_z(u):
            z_sb[u] = resident.tile([P, UNIT_TILES, K], BF16, name="z_sb")
            nc.sync.dma_start(out=z_sb[u][:, :, 0:N_X], in_=x_rows[:, unit_tiles(u), :])
            nc.sync.dma_start(out=z_sb[u][:, :, N_X:K], in_=hidden_rows[:, unit_tiles(u), :])

        def load_cell(u):
            cell_sb[u] = resident.tile([P, UNIT_TILES, N_H], BF16, name="cell_sb")
            nc.sync.dma_start(out=cell_sb[u][:], in_=cell_rows[:, unit_tiles(u), :])

        ones = consts.tile([P, 2 * P], BF16)
        nc.vector.memset(ones[:], 1.0)

        w_words = consts.tile([P, PASSES, 4, N_H], U32, align_bytes=64)
        w_scales = consts.tile([P, PASSES, 4, N_H], U8, align_bytes=64)
        nc.vector.memset(w_scales[:].rearrange("p g j n -> p (g j n)").bitcast(I32), 0)

        def load_weight(gate, words, scales):
            nc.sync.dma_start(
                out=w_words[:, :, gate, :].bitcast(I32),
                in_=words.rearrange("g p n t -> p g (n t)").bitcast(I32),
            )
            for r in range(SCALE_ROWS):
                nc.sync.dma_start(
                    out=w_scales[r:P:QUADRANT, :, gate, :].bitcast(I32),
                    in_=scales[:, r : P // BLOCK_PARTITIONS : SCALE_ROWS, :]
                    .rearrange("g q n -> q g n")
                    .bitcast(I32),
                )

        ident = consts.tile([P, P], F32)
        masks.make_identity(nc, ident[:])
        bias_rows = consts.tile([P, P], F32)
        nc.vector.memset(bias_rows[:], 0.0)
        bias_first_row = consts.tile([P, 2 * N_H], BF16)
        nc.vector.memset(bias_first_row[:], 0.0)
        warm = consts.tile([P, 1], F32)
        nc.vector.memset(warm[:], 0.0)
        nc.scalar.activation(out=warm[:], in_=warm[:], func=ACT.Sigmoid)

        bias_fo = consts.tile([2 * HALVES, P], BF16)
        nc.gpsimd.dma_start(out=bias_fo[0:HALVES, :], in_=bf1.rearrange("(h n) -> h n", h=HALVES))
        nc.gpsimd.dma_start(
            out=bias_fo[HALVES : 2 * HALVES, :], in_=bo1.rearrange("(h n) -> h n", h=HALVES)
        )
        bias_ic = consts.tile([1, 2 * N_H], BF16)
        nc.gpsimd.dma_start(out=bias_ic[:, 0:N_H], in_=bi1.rearrange("(o n) -> o n", o=1))
        nc.gpsimd.dma_start(out=bias_ic[:, N_H : 2 * N_H], in_=bc1.rearrange("(o n) -> o n", o=1))
        load_z(0)
        load_z(1)
        load_weight(FORGET, Wf1_words, Wf1_scales)
        load_weight(OUTPUT, Wo1_words, Wo1_scales)
        load_weight(INPUT, Wi1_words, Wi1_scales)
        load_weight(CAND, Wc1_words, Wc1_scales)
        for u in range(2, UNITS):
            load_z(u)
            load_cell(u - 2)
        load_cell(UNITS - 2)
        load_cell(UNITS - 1)

        bias_col = consts.tile([P, 2 * HALVES], F32)
        bias_all_rows = consts.tile([P, 2 * N_H], F32)

        def prepare_biases():
            nc.vector.tensor_copy(out=bias_rows[0 : 2 * HALVES, :], in_=bias_fo[:])
            bias_t = psum.tile([P, P], F32, tag="back")
            nc.tensor.transpose(bias_t[:], bias_rows[:], ident[:])
            nc.vector.tensor_copy(out=bias_col[:], in_=bias_t[:, 0 : 2 * HALVES])
            nc.vector.tensor_copy(out=bias_first_row[0:1, :], in_=bias_ic[:])
            bias_sum = psum.tile([P, 2 * N_H], F32, tag="back")
            nc.tensor.matmul(
                out=bias_sum[:], lhsT=ones[:, 0:P], rhs=bias_first_row[:], start=True, stop=True
            )
            nc.vector.tensor_copy(out=bias_all_rows[:], in_=bias_sum[:])

        def transpose_z(u):
            grouped[u] = work.tile(
                [P, PASSES, UNIT_ROWS, PACK], BF16, name="grouped", align_bytes=64
            )
            for r in range(UNIT_TILES):
                words = z_sb[u][:, r, :].bitcast(F32)
                z_t = psum.tile([P, PASSES, 2, P], F32, name="z_t")
                for g in range(PASSES):
                    for pair in range(2):
                        nc.tensor.transpose(
                            z_t[:, g, pair, :],
                            words[:, g * PASS_WORDS + pair : (g + 1) * PASS_WORDS : 2],
                            ident[:],
                        )
                copy_out = nc.scalar.copy if r % 2 == 0 else nc.vector.tensor_copy
                copy_out(
                    out=grouped[u][:, :, r * P : (r + 1) * P, :].bitcast(F32),
                    in_=z_t[:].rearrange("p g pair r -> p g r pair"),
                )

        def quantise_z(u):
            zq_words[u] = work.tile([P, PASSES, UNIT_ROWS], U32, name="zq_words", align_bytes=64)
            zq_scales[u] = work.tile([P, PASSES, UNIT_ROWS], U8, name="zq_scales", align_bytes=64)
            nc.vector.quantize_mx(
                out=zq_words[u][:].rearrange("p g r -> p (g r)").bitcast(FP8X4),
                scales=zq_scales[u][:].rearrange("p g r -> p (g r)"),
                in_=grouped[u][:].rearrange("p g r t -> p (g r t)"),
            )

        def multiply_features_on_partitions(u, gate):
            acc = psum.tile([P, HALVES, UNIT_ROWS], F32, name="acc_features")
            for h in range(HALVES):
                features = slice(h * P, (h + 1) * P)
                for g in range(PASSES):
                    nc.tensor.matmul_mx(
                        out=acc[:, h, :],
                        lhsT=w_words[:, g, gate, features].bitcast(FP8X4),
                        lhsT_scale=w_scales[:, g, gate, features],
                        rhs=zq_words[u][:, g, :].bitcast(FP8X4),
                        rhs_scale=zq_scales[u][:, g, :],
                        start=(g == 0),
                        stop=(g == PASSES - 1),
                    )
            return acc

        def sigmoid_features_on_partitions(u, gate, acc):
            for h in range(HALVES):
                column = gate * HALVES + h
                nc.scalar.activation(
                    out=sig_t[u][:, gate, h, :],
                    in_=acc[:, h, :],
                    func=ACT.Sigmoid,
                    bias=bias_col[:, column : column + 1],
                )

        def gates_with_features_on_partitions(u):
            sig_t[u] = work.tile([P, 2, HALVES, UNIT_ROWS], F32, name="sig_t")
            if u == 0:
                acc_forget = multiply_features_on_partitions(u, FORGET)
                acc_output = multiply_features_on_partitions(u, OUTPUT)
                prepare_biases()
                sigmoid_features_on_partitions(u, FORGET, acc_forget)
                sigmoid_features_on_partitions(u, OUTPUT, acc_output)
            else:
                for gate in (FORGET, OUTPUT):
                    acc = multiply_features_on_partitions(u, gate)
                    sigmoid_features_on_partitions(u, gate, acc)

        def gates_with_rows_on_partitions(u):
            pre[u] = work.tile([P, UNIT_TILES, 2 * N_H], F32, name="pre")
            for r in range(UNIT_TILES):
                rows = slice(r * P, (r + 1) * P)
                acc = psum.tile([P, 2 * N_H], F32, name="acc_rows")
                for g in range(PASSES):
                    nc.tensor.matmul_mx(
                        out=acc[:],
                        lhsT=zq_words[u][:, g, rows].bitcast(FP8X4),
                        lhsT_scale=zq_scales[u][:, g, rows],
                        rhs=w_words[:, g, INPUT : CAND + 1, :]
                        .rearrange("p j n -> p (j n)")
                        .bitcast(FP8X4),
                        rhs_scale=w_scales[:, g, INPUT : CAND + 1, :].rearrange("p j n -> p (j n)"),
                        start=(g == 0),
                        stop=(g == PASSES - 1),
                    )
                if u == UNITS - 1:
                    halves = (slice(N_H, 2 * N_H), slice(0, N_H))
                else:
                    halves = (slice(0, 2 * N_H),)
                for columns in halves:
                    nc.vector.tensor_tensor(
                        out=pre[u][:, r, columns],
                        in0=acc[:, columns],
                        in1=bias_all_rows[:, columns],
                        op=ALU.add,
                    )

        def finish_row_tile(u, r):
            if r == 0:
                in_gate[u] = work.tile([P, UNIT_TILES, N_H], F32, name="in_gate")
                cand[u] = work.tile([P, UNIT_TILES, N_H], F32, name="cand")
                tanh_cand[u] = work.tile([P, UNIT_TILES, N_H], F32, name="tanh_cand")
                h_new[u] = resident.tile([P, UNIT_TILES, N_H], F32, name="h_new")
                c_new[u] = resident.tile([P, UNIT_TILES, N_H], F32, name="c_new")
            last_unit = u == UNITS - 1
            last_tile = last_unit and r == UNIT_TILES - 1
            nc.scalar.activation(out=cand[u][:, r, :], in_=pre[u][:, r, N_H : 2 * N_H], func=ACT.Tanh)
            back = psum.tile([P, 2, HALVES, P], F32, name="back")
            for gate in (FORGET, OUTPUT):
                for h in range(HALVES):
                    nc.tensor.transpose(
                        back[:, gate, h, :], sig_t[u][:, gate, h, r * P : (r + 1) * P], ident[:]
                    )
            nc.vector.tensor_tensor(
                out=c_new[u][:, r, :],
                in0=back[:, FORGET, :, :].rearrange("p h n -> p (h n)"),
                in1=cell_sb[u][:, r, :],
                op=ALU.mult,
            )

            def input_gate_times_candidate(engine):
                nc.scalar.activation(
                    out=in_gate[u][:, r, :], in_=pre[u][:, r, 0:N_H], func=ACT.Sigmoid
                )
                engine.tensor_tensor(
                    out=in_gate[u][:, r, :], in0=in_gate[u][:, r, :], in1=cand[u][:, r, :], op=ALU.mult
                )

            def sum_for_c_new(engine):
                engine.tensor_tensor(
                    out=c_new[u][:, r, :], in0=c_new[u][:, r, :], in1=in_gate[u][:, r, :], op=ALU.add
                )
                if last_unit:
                    nc.sync.dma_start(out=c_rows[:, u * UNIT_TILES + r, :], in_=c_new[u][:, r, :])

            def output_gate_times_tanh():
                nc.scalar.activation(out=tanh_cand[u][:, r, :], in_=cand[u][:, r, :], func=ACT.Tanh)
                nc.vector.tensor_tensor(
                    out=h_new[u][:, r, :],
                    in0=back[:, OUTPUT, :, :].rearrange("p h n -> p (h n)"),
                    in1=tanh_cand[u][:, r, :],
                    op=ALU.mult,
                )
                if last_unit:
                    nc.sync.dma_start(out=h_rows[:, u * UNIT_TILES + r, :], in_=h_new[u][:, r, :])

            helper = nc.vector if last_tile else nc.gpsimd
            input_gate_times_candidate(helper)
            if last_unit:
                output_gate_times_tanh()
                sum_for_c_new(helper)
            else:
                sum_for_c_new(helper)
                output_gate_times_tanh()

        def store(u):
            nc.sync.dma_start(out=h_rows[:, unit_tiles(u), :], in_=h_new[u][:])
            nc.sync.dma_start(out=c_rows[:, unit_tiles(u), :], in_=c_new[u][:])

        transpose_z(0)
        quantise_z(0)
        for n in range(UNITS + 1):
            if n + 1 < UNITS:
                transpose_z(n + 1)
            if n >= 1:
                finish_row_tile(n - 1, 0)
            if n + 1 < UNITS:
                quantise_z(n + 1)
            if n >= 1:
                finish_row_tile(n - 1, 1)
            if 1 <= n < UNITS:
                store(n - 1)
            if n < UNITS:
                gates_with_features_on_partitions(n)
                gates_with_rows_on_partitions(n)
